import numpy as np
import ml_dtypes


def mxq(x, axis, fmt="e4m3"):
    dtype, down = {"e4m3": (ml_dtypes.float8_e4m3fn, 7), "e5m2": (ml_dtypes.float8_e5m2, 14)}[fmt]
    v = np.moveaxis(np.asarray(x, np.float32).astype(ml_dtypes.bfloat16).astype(np.float64), axis, -1)
    blocks = v.reshape(v.shape[:-1] + (-1, 32))
    amax = np.abs(blocks).max(-1, keepdims=True)
    byte = np.maximum(np.where(amax > 0, np.frexp(amax)[1] - 1 + 127, 0) - down, 1)
    scale = np.exp2(byte - 127.0)
    codes = (blocks / scale).astype(np.float32).astype(dtype).astype(np.float64)
    return np.moveaxis((codes * scale).reshape(v.shape), -1, axis)


WIDE = False


def mx_kscale(k):
    if not WIDE:
        return np.ones(k)
    levels = np.array([30, -30])
    if k % 512:
        return np.exp2(np.random.permutation(np.resize(levels, k // 32))).repeat(32)
    a = np.empty((k // 512, 16))
    for p in range(k // 512):
        a[p, :8] = np.random.permutation(np.resize(levels, 8))
        for g in range(8):
            far = levels[np.abs(levels - a[p, g]) >= 10]
            a[p, g + 8] = far[np.random.randint(len(far))]
    return np.exp2(a.ravel()).repeat(32)


BF16 = ml_dtypes.bfloat16


def bf(x):
    return np.asarray(x, np.float32).astype(BF16)


def f64(x):
    return np.asarray(x).astype(np.float64)


E2M1 = np.array([0.0, 0.5, 1.0, 1.5, 2.0, 3.0, 4.0, 6.0, -0.0, -0.5, -1.0, -1.5, -2.0, -3.0, -4.0, -6.0])


def pack_weight(w, fmt):
    k, n = w.shape
    w = f64(bf(w)).reshape(k // 32, 32, n)
    amax = np.abs(w).max(1)
    if fmt == "e4m3":
        byte = np.frexp(amax)[1] - 1 + 127 - 7
    else:
        mant, ex = np.frexp(amax / 6.0)
        byte = np.where(mant > 0.5, ex, ex - 1) + 127
    byte = np.clip(np.where(amax > 0, byte, 1), 1, 254)
    scaled = (w * np.exp2(127.0 - byte)[:, None, :]).reshape(k, n).astype(np.float32)
    by_word = np.ascontiguousarray(scaled.reshape(k // 512, 128, 4, n).transpose(0, 1, 3, 2))
    if fmt == "e4m3":
        words = by_word.astype(ml_dtypes.float8_e4m3fn).view(np.uint8)
    else:
        c = by_word.astype(ml_dtypes.float4_e2m1fn).view(np.uint8) & 0xF
        words = c[..., 0::2] | (c[..., 1::2] << 4)
    return np.ascontiguousarray(words), np.ascontiguousarray(byte.astype(np.uint8).reshape(k // 512, 16, n))


def unpack_weight(words, scales, fmt):
    g, p, n, _ = words.shape
    if fmt == "e4m3":
        vals = np.ascontiguousarray(words).view(ml_dtypes.float8_e4m3fn).astype(np.float64)
    else:
        nib = np.empty((g, p, n, 4), np.uint8)
        nib[..., 0::2] = words & 0xF
        nib[..., 1::2] = words >> 4
        vals = E2M1[nib]
    vals = vals * np.repeat(np.exp2(scales.astype(np.float64) - 127.0), 8, axis=1)[..., None]
    return vals.transpose(0, 1, 3, 2).reshape(g * 512, n)

def pack4(w):
    words, scales = pack_weight(w, "e2m1")
    return words.reshape(words.shape[0], 128, -1), scales


def unpack4(words, scales):
    return unpack_weight(words.reshape(words.shape[0], 128, -1, 2), scales, "e2m1")


B, S, DIM, H, HD = 4, 128, 2048, 16, 128
E = H * HD


def rope_tables():
    inv_freq = 1.0 / (10000.0 ** (np.arange(0, HD, 2) / HD))
    freqs = np.outer(np.arange(S), inv_freq)
    emb = np.concatenate([freqs, freqs], axis=-1)
    return np.cos(emb)[None, None], np.sin(emb)[None, None]


def rotate_half(x):
    x1, x2 = np.split(x, 2, axis=-1)
    return np.concatenate([-x2, x1], axis=-1)


def setup_inputs():
    s = mx_kscale(DIM)
    cos, sin = rope_tables()
    query = bf(np.random.standard_normal((B, S, DIM)) * s)
    wq_words, wq_scales = pack4((np.random.standard_normal((E, DIM)) / np.sqrt(DIM) / s).T)
    return {"query": query,
            "wq_words": wq_words, "wq_scales": wq_scales,
            "bq": bf(np.random.standard_normal(E) * 0.1),
            "cos": bf(cos), "sin": bf(sin)}


def reference(query, wq_words, wq_scales, bq, cos, sin):
    q = (mxq(f64(query), 2, "e5m2") @ unpack4(wq_words, wq_scales)) + f64(bq)
    q = q.reshape(B, S, H, HD).transpose(0, 2, 1, 3)
    return q * f64(cos) + rotate_half(q) * f64(sin)

@@ -1,0 +1,204 @@
+from contextlib import ExitStack
+
+import concourse.mybir as mybir
+from concourse.masks import make_identity
+
+B, S, DIM, H, HD = 4, 128, 2048, 16, 128
+E = H * HD
+FLOPS = 2 * B * S * DIM * E
+
+F32 = mybir.dt.float32
+BF16 = mybir.dt.bfloat16
+I32 = mybir.dt.int32
+U32 = mybir.dt.uint32
+U8 = mybir.dt.uint8
+FP8X4 = mybir.dt.float8_e5m2_x4
+FP4X4 = mybir.dt.float4_e2m1fn_x4
+ADD = mybir.AluOpType.add
+MULT = mybir.AluOpType.mult
+
+P = 128
+PASSES = DIM // 512
+CHUNK = 512
+CHUNKS = E // CHUNK
+HEADS = CHUNK // HD
+HALF = HD // 2
+V_HEADS = HEADS - 1
+
+
+def tile_attention_pa_kernel(tc, query, wq_words, wq_scales, bq, cos, sin, out):
+    nc = tc.nc
+
+    with ExitStack() as ctx:
+        keep = ctx.enter_context(tc.tile_pool(name="keep", bufs=1))
+        work = ctx.enter_context(tc.tile_pool(name="work", bufs=3))
+        psum_keep = ctx.enter_context(tc.psum_pool(name="psum_keep", bufs=1))
+        psum_turn = ctx.enter_context(tc.psum_pool(name="psum_turn", bufs=3))
+        psum_acc = ctx.enter_context(tc.psum_pool(name="psum_acc", bufs=4))
+        ctx.enter_context(tc.manual_schedule())
+
+        w_scales = [keep.tile([P, PASSES, CHUNK], U8, name="w_scales%d" % c, align_bytes=64) for c in range(CHUNKS)]
+        w_codes = [
+            [keep.tile([P, 2, 2 * CHUNK], U8, name="w_codes%d_%d" % (c, j), align_bytes=64) for j in range(2)]
+            for c in range(CHUNKS)
+        ]
+        q_rows = [
+            [keep.tile([P, DIM // 2], BF16, name="q_rows%d_%d" % (b, j), align_bytes=64) for j in range(2)]
+            for b in range(B)
+        ]
+        q_grouped = [keep.tile([P, PASSES * S * 4], BF16, name="q_grouped%d" % b, align_bytes=64) for b in range(B)]
+        q_codes = [keep.tile([P, PASSES * S], U32, name="q_codes%d" % b, align_bytes=64) for b in range(B)]
+        q_scales = [keep.tile([P, PASSES * S], U8, name="q_scales%d" % b, align_bytes=64) for b in range(B)]
+        bias = [keep.tile([P, CHUNK], BF16, name="bias%d" % c, align_bytes=64) for c in range(CHUNKS)]
+        bias_rows = keep.tile([P, CHUNK], BF16, align_bytes=64)
+        tables = keep.tile([P, 2, HD], BF16, align_bytes=64)
+        ident_f32 = keep.tile([P, P], F32, align_bytes=64)
+        ident_bf16 = keep.tile([P, P], BF16, align_bytes=64)
+        tables_ps = psum_keep.tile([P, 2, HD], F32)
+
+        nc.vector.memset(w_scales[0][:].bitcast(I32), 0)
+        nc.vector.memset(bias_rows[:].bitcast(I32), 0)
+        for c in range(1, CHUNKS):
+            nc.vector.memset(w_scales[c][:].bitcast(I32), 0)
+        make_identity(nc, ident_f32[:])
+        make_identity(nc, ident_bf16[:])
+
+        nc.scalar.dma_start(out=tables[:, 1, :], in_=sin[0, 0])
+        nc.scalar.dma_start(out=tables[:, 0, :], in_=cos[0, 0])
+        nc.scalar.dma_start(out=bias_rows[0:CHUNKS, :], in_=bq.rearrange("(c n) -> c n", n=CHUNK))
+        nc.gpsimd.tensor_scalar(
+            out=tables[:, 1, 0:HALF], in0=tables[:, 1, 0:HALF], scalar1=-1.0, scalar2=0.0, op0=MULT, op1=ADD
+        )
+
+        for n in range(B):
+            for j in range(2):
+                nc.sync.dma_start(out=q_rows[n][j][:], in_=query[n, :, j * DIM // 2 : (j + 1) * DIM // 2])
+            for quad in range(4):
+                nc.sync.dma_start(
+                    out=w_scales[n][32 * quad : 32 * quad + 4, :, :].bitcast(I32),
+                    in_=wq_scales[:, 4 * quad : 4 * quad + 4, n * CHUNK : (n + 1) * CHUNK]
+                    .rearrange("g r n -> r g n")
+                    .bitcast(I32),
+                )
+            for j in range(2):
+                nc.sync.dma_start(
+                    out=w_codes[n][j][:].bitcast(I32),
+                    in_=wq_words[2 * j : 2 * j + 2, :, 2 * n * CHUNK : 2 * (n + 1) * CHUNK]
+                    .rearrange("g p n -> p g n")
+                    .bitcast(I32),
+                )
+
+        def turn_query(b):
+            for j in range(2):
+                words = q_rows[b][j][:].bitcast(F32)
+                turned = psum_turn.tile([P, 2, 2, S], F32, tag="turn")
+                for g in range(2):
+                    for u in range(2):
+                        nc.tensor.transpose(
+                            turned[:, g, u, :], words[:, 256 * g + u : 256 * (g + 1) : 2], ident_f32[:]
+                        )
+                nc.scalar.copy(
+                    out=q_grouped[b][:, j * 1024 : (j + 1) * 1024]
+                    .bitcast(F32)
+                    .rearrange("p (g s u) -> p g s u", g=2, u=2),
+                    in_=turned[:].rearrange("p g u s -> p g s u"),
+                )
+
+        def spread_bias(c):
+            spread = psum_turn.tile([P, CHUNK], BF16, tag="turn")
+            nc.tensor.matmul(
+                spread[:], lhsT=ident_bf16[:, c : c + 1].to_broadcast([P, P]), rhs=bias_rows[:], start=True, stop=True
+            )
+            nc.scalar.copy(out=bias[c][:], in_=spread[:])
+
+        def quantize(b, pieces):
+            width = PASSES * S // pieces
+            for j in range(pieces):
+                nc.vector.quantize_mx(
+                    out=q_codes[b][:, j * width : (j + 1) * width].bitcast(FP8X4),
+                    scales=q_scales[b][:, j * width : (j + 1) * width],
+                    in_=q_grouped[b][:, 4 * j * width : 4 * (j + 1) * width],
+                )
+
+        def project(b, c):
+            acc = psum_acc.tile([P, CHUNK], F32, tag="acc")
+            for g in range(PASSES):
+                nc.tensor.matmul_mx(
+                    out=acc[:],
+                    lhsT=q_codes[b][:, g * S : (g + 1) * S].bitcast(FP8X4),
+                    lhsT_scale=q_scales[b][:, g * S : (g + 1) * S],
+                    rhs=w_codes[c][g // 2][:, g % 2, :].bitcast(FP4X4),
+                    rhs_scale=w_scales[c][:, g, :],
+                    start=(g == 0),
+                    stop=(g == PASSES - 1),
+                )
+            return acc
+
+        def add_bias(acc, c):
+            q = work.tile([P, HEADS, HD], F32, tag="q")
+            q_cos = work.tile([P, HEADS, HD], F32, tag="q_cos")
+            nc.vector.tensor_tensor(out=q[:].rearrange("p h d -> p (h d)"), in0=acc[:], in1=bias[c][:], op=ADD)
+            nc.gpsimd.tensor_tensor(out=q_cos[:, V_HEADS, :], in0=q[:, V_HEADS, :], in1=tables[:, 0, :], op=MULT)
+            return q, q_cos
+
+        def times_cos(q, q_cos):
+            nc.vector.tensor_tensor(
+                out=q_cos[:, 0:V_HEADS, :],
+                in0=q[:, 0:V_HEADS, :],
+                in1=tables_ps[:, 0:1, :].to_broadcast([P, V_HEADS, HD]),
+                op=MULT,
+            )
+
+        def finish(b, c, q, q_cos, adder):
+            q_sin = work.tile([P, HEADS, HD], F32, tag="q_sin")
+            result = work.tile([P, HEADS, HD], F32, tag="result")
+            nc.vector.tensor_tensor(
+                out=q_sin[:].rearrange("p h (t d) -> p h t d", t=2),
+                in0=q[:].rearrange("p h (t d) -> p h t d", t=2)[:, :, ::-1, :],
+                in1=tables_ps[:, 1:2, :].rearrange("p o (t d) -> p o t d", t=2).to_broadcast([P, HEADS, 2, HALF]),
+                op=MULT,
+            )
+            adder.tensor_tensor(
+                out=result[:].rearrange("p h d -> p (h d)"),
+                in0=q_cos[:].rearrange("p h d -> p (h d)"),
+                in1=q_sin[:].rearrange("p h d -> p (h d)"),
+                op=ADD,
+            )
+            nc.sync.dma_start(
+                out=out[b, c * HEADS : (c + 1) * HEADS, :, :].rearrange("h s d -> s h d"), in_=result[:]
+            )
+
+        tiles = []
+        for n in range(B):
+            tiles.extend([(b, n) for b in range(n)])
+            tiles.extend([(n, c) for c in range(n + 1)])
+
+        turn_query(0)
+        nc.tensor.matmul(
+            tables_ps[:].rearrange("p t d -> p (t d)"),
+            lhsT=ident_bf16[:],
+            rhs=tables[:].rearrange("p t d -> p (t d)"),
+            start=True,
+            stop=True,
+        )
+        spread_bias(0)
+        quantize(0, 2)
+
+        waiting = None
+        for i, (b, c) in enumerate(tiles):
+            acc = project(b, c)
+            if b == c and b + 1 < B:
+                turn_query(b + 1)
+                spread_bias(b + 1)
+            q, q_cos = add_bias(acc, c)
+            if waiting is not None:
+                finish(*waiting, nc.gpsimd)
+                if waiting[0] == waiting[1]:
+                    quantize(waiting[0] + 1, 1)
+            times_cos(q, q_cos)
+            waiting = (b, c, q, q_cos)
+            if i == 0:
+                finish(*waiting, nc.gpsimd)
+                quantize(1, 2)
+                waiting = None
+        finish(*waiting, nc.vector)

@@ -16,14 +16,17 @@ FP8X4 = mybir.dt.float8_e5m2_x4
 FP4X4 = mybir.dt.float4_e2m1fn_x4
 ADD = mybir.AluOpType.add
 MULT = mybir.AluOpType.mult
+IDENTITY = mybir.ActivationFunctionType.Identity
 
 P = 128
 PASSES = DIM // 512
-CHUNK = 512
-CHUNKS = E // CHUNK
-HEADS = CHUNK // HD
+BANK = 512
+GROUP = BANK // HD
 HALF = HD // 2
-V_HEADS = HEADS - 1
+CHUNKS = E // BANK
+ROW_CHUNKS = 2
+ROW_HEADS = ROW_CHUNKS * GROUP
+COL_HEADS = H - ROW_HEADS
 
 
 def tile_attention_pa_kernel(tc, query, wq_words, wq_scales, bq, cos, sin, out):
@@ -31,149 +34,211 @@ def tile_attention_pa_kernel(tc, query, wq_words, wq_scales, bq, cos, sin, out):
 
     with ExitStack() as ctx:
         keep = ctx.enter_context(tc.tile_pool(name="keep", bufs=1))
-        work = ctx.enter_context(tc.tile_pool(name="work", bufs=3))
+        work = ctx.enter_context(tc.tile_pool(name="work", bufs=4))
         psum_keep = ctx.enter_context(tc.psum_pool(name="psum_keep", bufs=1))
         psum_turn = ctx.enter_context(tc.psum_pool(name="psum_turn", bufs=3))
         psum_acc = ctx.enter_context(tc.psum_pool(name="psum_acc", bufs=4))
         ctx.enter_context(tc.manual_schedule())
 
-        w_scales = [keep.tile([P, PASSES, CHUNK], U8, name="w_scales%d" % c, align_bytes=64) for c in range(CHUNKS)]
-        w_codes = [
-            [keep.tile([P, 2, 2 * CHUNK], U8, name="w_codes%d_%d" % (c, j), align_bytes=64) for j in range(2)]
-            for c in range(CHUNKS)
-        ]
-        q_rows = [
-            [keep.tile([P, DIM // 2], BF16, name="q_rows%d_%d" % (b, j), align_bytes=64) for j in range(2)]
-            for b in range(B)
-        ]
-        q_grouped = [keep.tile([P, PASSES * S * 4], BF16, name="q_grouped%d" % b, align_bytes=64) for b in range(B)]
-        q_codes = [keep.tile([P, PASSES * S], U32, name="q_codes%d" % b, align_bytes=64) for b in range(B)]
-        q_scales = [keep.tile([P, PASSES * S], U8, name="q_scales%d" % b, align_bytes=64) for b in range(B)]
-        bias = [keep.tile([P, CHUNK], BF16, name="bias%d" % c, align_bytes=64) for c in range(CHUNKS)]
-        bias_rows = keep.tile([P, CHUNK], BF16, align_bytes=64)
+        row_scales = [keep.tile([P, PASSES, BANK], U8, name="row_scales%d" % c, align_bytes=64) for c in range(ROW_CHUNKS)]
+        col_scales = keep.tile([P, PASSES, COL_HEADS * HD], U8, align_bytes=64)
+        w_codes = [keep.tile([P, PASSES, 2 * BANK], U8, name="w_codes%d" % c, align_bytes=64) for c in range(CHUNKS)]
+        q_rows = [keep.tile([P, DIM], BF16, name="q_rows%d" % b, align_bytes=64) for b in range(B)]
+        q_grouped = keep.tile([P, PASSES, B * S * 4], BF16, align_bytes=64)
+        q_codes = keep.tile([P, PASSES, B * S], U32, align_bytes=64)
+        q_scales = keep.tile([P, PASSES, B * S], U8, align_bytes=64)
+        row_bias = [keep.tile([P, BANK], BF16, name="row_bias%d" % c, align_bytes=64) for c in range(ROW_CHUNKS)]
+        col_bias = keep.tile([P, COL_HEADS], F32, align_bytes=64)
+        bias_rows = keep.tile([P, HD], BF16, align_bytes=64)
         tables = keep.tile([P, 2, HD], BF16, align_bytes=64)
         ident_f32 = keep.tile([P, P], F32, align_bytes=64)
         ident_bf16 = keep.tile([P, P], BF16, align_bytes=64)
         tables_ps = psum_keep.tile([P, 2, HD], F32)
 
-        nc.vector.memset(w_scales[0][:].bitcast(I32), 0)
         nc.vector.memset(bias_rows[:].bitcast(I32), 0)
-        for c in range(1, CHUNKS):
-            nc.vector.memset(w_scales[c][:].bitcast(I32), 0)
+        nc.vector.memset(row_scales[0][:].bitcast(I32), 0)
         make_identity(nc, ident_f32[:])
-        make_identity(nc, ident_bf16[:])
+        nc.vector.memset(row_scales[1][:].bitcast(I32), 0)
+        nc.vector.tensor_copy(out=ident_bf16[:], in_=ident_f32[:])
+        nc.vector.memset(col_scales[:].bitcast(I32), 0)
 
-        nc.scalar.dma_start(out=tables[:, 1, :], in_=sin[0, 0])
-        nc.scalar.dma_start(out=tables[:, 0, :], in_=cos[0, 0])
-        nc.scalar.dma_start(out=bias_rows[0:CHUNKS, :], in_=bq.rearrange("(c n) -> c n", n=CHUNK))
-        nc.gpsimd.tensor_scalar(
-            out=tables[:, 1, 0:HALF], in0=tables[:, 1, 0:HALF], scalar1=-1.0, scalar2=0.0, op0=MULT, op1=ADD
-        )
+        def load_query(b, pieces):
+            for j in range(pieces):
+                cols = slice(j * DIM // pieces, (j + 1) * DIM // pieces)
+                nc.sync.dma_start(out=q_rows[b][:, cols], in_=query[b, :, cols])
 
-        for n in range(B):
-            for j in range(2):
-                nc.sync.dma_start(out=q_rows[n][j][:], in_=query[n, :, j * DIM // 2 : (j + 1) * DIM // 2])
+        def load_scales(plane, first, count):
             for quad in range(4):
                 nc.sync.dma_start(
-                    out=w_scales[n][32 * quad : 32 * quad + 4, :, :].bitcast(I32),
-                    in_=wq_scales[:, 4 * quad : 4 * quad + 4, n * CHUNK : (n + 1) * CHUNK]
+                    out=plane[32 * quad : 32 * quad + 4, :, :].bitcast(I32),
+                    in_=wq_scales[:, 4 * quad : 4 * quad + 4, first * BANK : (first + count) * BANK]
                     .rearrange("g r n -> r g n")
                     .bitcast(I32),
                 )
-            for j in range(2):
-                nc.sync.dma_start(
-                    out=w_codes[n][j][:].bitcast(I32),
-                    in_=wq_words[2 * j : 2 * j + 2, :, 2 * n * CHUNK : 2 * (n + 1) * CHUNK]
-                    .rearrange("g p n -> p g n")
-                    .bitcast(I32),
-                )
 
-        def turn_query(b):
-            for j in range(2):
-                words = q_rows[b][j][:].bitcast(F32)
-                turned = psum_turn.tile([P, 2, 2, S], F32, tag="turn")
-                for g in range(2):
-                    for u in range(2):
-                        nc.tensor.transpose(
-                            turned[:, g, u, :], words[:, 256 * g + u : 256 * (g + 1) : 2], ident_f32[:]
-                        )
-                nc.scalar.copy(
-                    out=q_grouped[b][:, j * 1024 : (j + 1) * 1024]
-                    .bitcast(F32)
-                    .rearrange("p (g s u) -> p g s u", g=2, u=2),
-                    in_=turned[:].rearrange("p g u s -> p g s u"),
-                )
-
-        def spread_bias(c):
-            spread = psum_turn.tile([P, CHUNK], BF16, tag="turn")
-            nc.tensor.matmul(
-                spread[:], lhsT=ident_bf16[:, c : c + 1].to_broadcast([P, P]), rhs=bias_rows[:], start=True, stop=True
-            )
-            nc.scalar.copy(out=bias[c][:], in_=spread[:])
-
-        def quantize(b, pieces):
-            width = PASSES * S // pieces
+        def load_codes(c, pieces):
             for j in range(pieces):
-                nc.vector.quantize_mx(
-                    out=q_codes[b][:, j * width : (j + 1) * width].bitcast(FP8X4),
-                    scales=q_scales[b][:, j * width : (j + 1) * width],
-                    in_=q_grouped[b][:, 4 * j * width : 4 * (j + 1) * width],
+                passes = slice(j * PASSES // pieces, (j + 1) * PASSES // pieces)
+                nc.sync.dma_start(
+                    out=w_codes[c][:, passes, :].bitcast(I32),
+                    in_=wq_words[passes, :, 2 * c * BANK : 2 * (c + 1) * BANK].rearrange("g p n -> p g n").bitcast(I32),
                 )
 
-        def project(b, c):
-            acc = psum_acc.tile([P, CHUNK], F32, tag="acc")
+        load_query(0, 2)
+        nc.sync.dma_start(out=bias_rows[0:H, :], in_=bq.rearrange("(h d) -> h d", d=HD))
+        load_scales(row_scales[0], 0, 1)
+        load_codes(0, 2)
+        nc.sync.dma_start(out=tables[:, 1, :], in_=sin[0, 0])
+        nc.sync.dma_start(out=tables[:, 0, :], in_=cos[0, 0])
+        nc.gpsimd.tensor_scalar(
+            out=tables[:, 1, 0:HALF], in0=tables[:, 1, 0:HALF], scalar1=-1.0, scalar2=0.0, op0=MULT, op1=ADD
+        )
+        load_query(1, 1)
+        load_scales(row_scales[1], 1, 1)
+        load_codes(1, 1)
+        for b in range(2, B):
+            load_query(b, 1)
+        load_scales(col_scales, ROW_CHUNKS, CHUNKS - ROW_CHUNKS)
+        for c in range(ROW_CHUNKS, CHUNKS):
+            load_codes(c, 1)
+
+        grouped_words = q_grouped[:].bitcast(F32).rearrange("p g (b s u) -> p g b s u", b=B, u=2)
+
+        def turn_query(b, first, count):
+            words = q_rows[b][:].bitcast(F32)
+            turned = psum_turn.tile([P, count, 2, S], F32, tag="turn")
+            for j in range(count):
+                g = first + j
+                for u in range(2):
+                    nc.tensor.transpose(turned[:, j, u, :], words[:, 256 * g + u : 256 * (g + 1) : 2], ident_f32[:])
+            nc.scalar.copy(
+                out=grouped_words[:, first : first + count, b], in_=turned[:].rearrange("p j u s -> p j s u")
+            )
+
+        def turn_batch(b):
+            turn_query(b, 0, 2)
+            turn_query(b, 2, 2)
+
+        def quantize(b):
+            cols = slice(b * S, (b + 1) * S)
+            for g in range(PASSES):
+                nc.vector.quantize_mx(
+                    out=q_codes[:, g, cols].bitcast(FP8X4),
+                    scales=q_scales[:, g, cols],
+                    in_=q_grouped[:, g, 4 * b * S : 4 * (b + 1) * S],
+                )
+
+        def spread_row_bias(c):
+            spread = psum_acc.tile([P, GROUP, HD], BF16, tag="acc")
+            for hh in range(GROUP):
+                h = c * GROUP + hh
+                nc.tensor.matmul(
+                    spread[:, hh, :],
+                    lhsT=ident_bf16[:, h : h + 1].to_broadcast([P, P]),
+                    rhs=bias_rows[:],
+                    start=True,
+                    stop=True,
+                )
+            nc.scalar.copy(out=row_bias[c][:], in_=spread[:].rearrange("p h d -> p (h d)"))
+
+        def turn_col_bias():
+            turned = psum_acc.tile([P, COL_HEADS], F32, tag="acc")
+            nc.tensor.matmul(turned[:], lhsT=bias_rows[:], rhs=ident_bf16[:, ROW_HEADS:H], start=True, stop=True)
+            nc.scalar.copy(out=col_bias[:], in_=turned[:])
+
+        def project_rows(b, c):
+            acc = psum_acc.tile([P, BANK], F32, tag="acc")
             for g in range(PASSES):
                 nc.tensor.matmul_mx(
                     out=acc[:],
-                    lhsT=q_codes[b][:, g * S : (g + 1) * S].bitcast(FP8X4),
-                    lhsT_scale=q_scales[b][:, g * S : (g + 1) * S],
-                    rhs=w_codes[c][g // 2][:, g % 2, :].bitcast(FP4X4),
-                    rhs_scale=w_scales[c][:, g, :],
+                    lhsT=q_codes[:, g, b * S : (b + 1) * S].bitcast(FP8X4),
+                    lhsT_scale=q_scales[:, g, b * S : (b + 1) * S],
+                    rhs=w_codes[c][:, g, :].bitcast(FP4X4),
+                    rhs_scale=row_scales[c][:, g, :],
                     start=(g == 0),
                     stop=(g == PASSES - 1),
                 )
             return acc
 
-        def add_bias(acc, c):
-            q = work.tile([P, HEADS, HD], F32, tag="q")
-            q_cos = work.tile([P, HEADS, HD], F32, tag="q_cos")
-            nc.vector.tensor_tensor(out=q[:].rearrange("p h d -> p (h d)"), in0=acc[:], in1=bias[c][:], op=ADD)
-            nc.gpsimd.tensor_tensor(out=q_cos[:, V_HEADS, :], in0=q[:, V_HEADS, :], in1=tables[:, 0, :], op=MULT)
-            return q, q_cos
-
-        def times_cos(q, q_cos):
-            nc.vector.tensor_tensor(
-                out=q_cos[:, 0:V_HEADS, :],
-                in0=q[:, 0:V_HEADS, :],
-                in1=tables_ps[:, 0:1, :].to_broadcast([P, V_HEADS, HD]),
-                op=MULT,
+        def project_cols(j):
+            c, hh = divmod(ROW_HEADS + j, GROUP)
+            acc = psum_acc.tile([P, BANK], F32, tag="acc")
+            for g in range(PASSES):
+                nc.tensor.matmul_mx(
+                    out=acc[:],
+                    lhsT=w_codes[c][:, g, 2 * hh * HD : 2 * (hh + 1) * HD].bitcast(FP4X4),
+                    lhsT_scale=col_scales[:, g, j * HD : (j + 1) * HD],
+                    rhs=q_codes[:, g, :].bitcast(FP8X4),
+                    rhs_scale=q_scales[:, g, :],
+                    start=(g == 0),
+                    stop=(g == PASSES - 1),
+                )
+            q_cols = work.tile([P, B, S], F32, tag="q_cols")
+            nc.scalar.activation(
+                out=q_cols[:].rearrange("p b s -> p (b s)"), in_=acc[:], func=IDENTITY, bias=col_bias[:, j : j + 1]
             )
+            return q_cols
 
-        def finish(b, c, q, q_cos, adder):
-            q_sin = work.tile([P, HEADS, HD], F32, tag="q_sin")
-            result = work.tile([P, HEADS, HD], F32, tag="result")
+        def turn_back(q_cols):
+            q = psum_turn.tile([P, B, HD], F32, tag="turn")
+            for b in range(B):
+                nc.tensor.transpose(q[:, b, :], q_cols[:, b, :], ident_f32[:])
+            return q
+
+        def add_row_bias(acc, c):
+            q = work.tile([P, GROUP, HD], F32, tag="q")
+            nc.vector.tensor_tensor(out=q[:].rearrange("p h d -> p (h d)"), in0=acc[:], in1=row_bias[c][:], op=ADD)
+            return q
+
+        def times_cos(q, tabs):
+            q_cos = work.tile([P, GROUP, HD], F32, tag="q_cos")
+            nc.vector.tensor_tensor(
+                out=q_cos[:], in0=q[:], in1=tabs[:, 0:1, :].to_broadcast([P, GROUP, HD]), op=MULT
+            )
+            return q_cos
+
+        def times_sin(q, tabs):
+            q_sin = work.tile([P, GROUP, HD], F32, tag="q_sin")
             nc.vector.tensor_tensor(
                 out=q_sin[:].rearrange("p h (t d) -> p h t d", t=2),
                 in0=q[:].rearrange("p h (t d) -> p h t d", t=2)[:, :, ::-1, :],
-                in1=tables_ps[:, 1:2, :].rearrange("p o (t d) -> p o t d", t=2).to_broadcast([P, HEADS, 2, HALF]),
+                in1=tabs[:, 1:2, :].rearrange("p o (t d) -> p o t d", t=2).to_broadcast([P, GROUP, 2, HALF]),
                 op=MULT,
             )
+            return q_sin
+
+        def products(q, tabs):
+            return times_cos(q, tabs), times_sin(q, tabs)
+
+        def add_and_store(pair, target, adder):
+            result = work.tile([P, GROUP, HD], F32, tag="result")
             adder.tensor_tensor(
                 out=result[:].rearrange("p h d -> p (h d)"),
-                in0=q_cos[:].rearrange("p h d -> p (h d)"),
-                in1=q_sin[:].rearrange("p h d -> p (h d)"),
+                in0=pair[0][:].rearrange("p h d -> p (h d)"),
+                in1=pair[1][:].rearrange("p h d -> p (h d)"),
                 op=ADD,
             )
-            nc.sync.dma_start(
-                out=out[b, c * HEADS : (c + 1) * HEADS, :, :].rearrange("h s d -> s h d"), in_=result[:]
-            )
+            nc.sync.dma_start(out=target, in_=result[:])
 
-        tiles = []
-        for n in range(B):
-            tiles.extend([(b, n) for b in range(n)])
-            tiles.extend([(n, c) for c in range(n + 1)])
+        def row_target(b, c):
+            return out[b, c * GROUP : (c + 1) * GROUP, :, :].rearrange("h s d -> s h d")
 
-        turn_query(0)
+        def col_target(j):
+            return out[:, ROW_HEADS + j, :, :].rearrange("b s d -> s b d")
+
+        def finish_rows(q, b, c):
+            add_and_store(products(q, tables_ps), row_target(b, c), nc.gpsimd)
+
+        def finish_cols(q, j, adder):
+            add_and_store(products(q, tables), col_target(j), adder)
+
+        turn_query(0, 0, 2)
+        turn_query(0, 2, 1)
+        turn_query(0, 3, 1)
+        spread_row_bias(0)
+        spread_row_bias(1)
+        quantize(0)
+        acc = project_rows(0, 0)
         nc.tensor.matmul(
             tables_ps[:].rearrange("p t d -> p (t d)"),
             lhsT=ident_bf16[:],
@@ -181,24 +246,45 @@ def tile_attention_pa_kernel(tc, query, wq_words, wq_scales, bq, cos, sin, out):
             start=True,
             stop=True,
         )
-        spread_bias(0)
-        quantize(0, 2)
+        turn_batch(1)
+        first_pair = products(add_row_bias(acc, 0), tables_ps)
+        quantize(1)
 
+        for b, c, nxt in [(0, 1, 2), (1, 0, 3)]:
+            acc = project_rows(b, c)
+            turn_batch(nxt)
+            q = add_row_bias(acc, c)
+            if first_pair is not None:
+                add_and_store(first_pair, row_target(0, 0), nc.vector)
+                first_pair = None
+            q_cos = times_cos(q, tables_ps)
+            quantize(nxt)
+            add_and_store((q_cos, times_sin(q, tables_ps)), row_target(b, c), nc.gpsimd)
+        turn_col_bias()
+
+        lead = [(1, 1), (2, 0)]
+        rest = [(2, 1), (3, 0), (3, 1)]
         waiting = None
-        for i, (b, c) in enumerate(tiles):
-            acc = project(b, c)
-            if b == c and b + 1 < B:
-                turn_query(b + 1)
-                spread_bias(b + 1)
-            q, q_cos = add_bias(acc, c)
+        for b, c in lead:
+            q = add_row_bias(project_rows(b, c), c)
             if waiting is not None:
-                finish(*waiting, nc.gpsimd)
-                if waiting[0] == waiting[1]:
-                    quantize(waiting[0] + 1, 1)
-            times_cos(q, q_cos)
-            waiting = (b, c, q, q_cos)
-            if i == 0:
-                finish(*waiting, nc.gpsimd)
-                quantize(1, 2)
+                finish_rows(*waiting)
+            waiting = (q, b, c)
+
+        for k in range(COL_HEADS // 2):
+            heads = (2 * k, 2 * k + 1)
+            q_cols = [project_cols(j) for j in heads]
+            if waiting is not None:
+                finish_rows(*waiting)
                 waiting = None
-        finish(*waiting, nc.vector)
+            if k < len(rest):
+                b, c = rest[k]
+                waiting = (add_row_bias(project_rows(b, c), c), b, c)
+            turned = [turn_back(x) for x in q_cols]
+            if k < len(rest):
+                for j in range(2):
+                    finish_cols(turned[j], heads[j], nc.gpsimd)
+            else:
+                pairs = [products(x, tables) for x in turned]
+                for j in range(2):
+                    add_and_store(pairs[j], col_target(heads[j]), nc.vector)

@@ -55,6 +55,8 @@ def tile_attention_pa_kernel(tc, query, wq_words, wq_scales, bq, cos, sin, out):
         ident_bf16 = keep.tile([P, P], BF16, align_bytes=64)
         tables_ps = psum_keep.tile([P, 2, HD], F32)
 
+        zeros = keep.tile([P, BANK], BF16, align_bytes=64)
+        nc.vector.memset(zeros[:].bitcast(I32), 0)
         nc.vector.memset(bias_rows[:].bitcast(I32), 0)
         nc.vector.memset(row_scales[0][:].bitcast(I32), 0)
         make_identity(nc, ident_f32[:])
@@ -86,18 +88,18 @@ def tile_attention_pa_kernel(tc, query, wq_words, wq_scales, bq, cos, sin, out):
 
         load_query(0, 2)
         nc.sync.dma_start(out=bias_rows[0:H, :], in_=bq.rearrange("(h d) -> h d", d=HD))
-        load_scales(row_scales[0], 0, 1)
-        load_codes(0, 2)
         nc.sync.dma_start(out=tables[:, 1, :], in_=sin[0, 0])
-        nc.sync.dma_start(out=tables[:, 0, :], in_=cos[0, 0])
-        nc.gpsimd.tensor_scalar(
-            out=tables[:, 1, 0:HALF], in0=tables[:, 1, 0:HALF], scalar1=-1.0, scalar2=0.0, op0=MULT, op1=ADD
+        nc.vector.tensor_scalar(
+            out=tables[:, 1, 0:HALF], in0=tables[:, 1, 0:HALF], scalar1=-1.0, scalar2=None, op0=MULT
         )
         load_query(1, 1)
+        load_scales(row_scales[0], 0, 1)
+        load_codes(0, 2)
+        nc.sync.dma_start(out=tables[:, 0, :], in_=cos[0, 0])
+        load_query(2, 1)
         load_scales(row_scales[1], 1, 1)
         load_codes(1, 1)
-        for b in range(2, B):
-            load_query(b, 1)
+        load_query(3, 1)
         load_scales(col_scales, ROW_CHUNKS, CHUNKS - ROW_CHUNKS)
         for c in range(ROW_CHUNKS, CHUNKS):
             load_codes(c, 1)
@@ -146,15 +148,16 @@ def tile_attention_pa_kernel(tc, query, wq_words, wq_scales, bq, cos, sin, out):
             nc.tensor.matmul(turned[:], lhsT=bias_rows[:], rhs=ident_bf16[:, ROW_HEADS:H], start=True, stop=True)
             nc.scalar.copy(out=col_bias[:], in_=turned[:])
 
-        def project_rows(b, c):
-            acc = psum_acc.tile([P, BANK], F32, tag="acc")
+        def project_rows(b, first, count):
+            c, hh = divmod(first, GROUP)
+            acc = psum_acc.tile([P, count * HD], F32, tag="acc")
             for g in range(PASSES):
                 nc.tensor.matmul_mx(
                     out=acc[:],
                     lhsT=q_codes[:, g, b * S : (b + 1) * S].bitcast(FP8X4),
                     lhsT_scale=q_scales[:, g, b * S : (b + 1) * S],
-                    rhs=w_codes[c][:, g, :].bitcast(FP4X4),
-                    rhs_scale=row_scales[c][:, g, :],
+                    rhs=w_codes[c][:, g, 2 * hh * HD : 2 * (hh + count) * HD].bitcast(FP4X4),
+                    rhs_scale=row_scales[c][:, g, hh * HD : (hh + count) * HD],
                     start=(g == 0),
                     stop=(g == PASSES - 1),
                 )
@@ -185,106 +188,125 @@ def tile_attention_pa_kernel(tc, query, wq_words, wq_scales, bq, cos, sin, out):
                 nc.tensor.transpose(q[:, b, :], q_cols[:, b, :], ident_f32[:])
             return q
 
-        def add_row_bias(acc, c):
-            q = work.tile([P, GROUP, HD], F32, tag="q")
-            nc.vector.tensor_tensor(out=q[:].rearrange("p h d -> p (h d)"), in0=acc[:], in1=row_bias[c][:], op=ADD)
-            return q
-
-        def times_cos(q, tabs):
-            q_cos = work.tile([P, GROUP, HD], F32, tag="q_cos")
+        def add_row_bias(acc, first, count):
+            c, hh = divmod(first, GROUP)
+            q = work.tile([P, count, HD], F32, tag="q")
             nc.vector.tensor_tensor(
-                out=q_cos[:], in0=q[:], in1=tabs[:, 0:1, :].to_broadcast([P, GROUP, HD]), op=MULT
-            )
-            return q_cos
-
-        def times_sin(q, tabs):
-            q_sin = work.tile([P, GROUP, HD], F32, tag="q_sin")
-            nc.vector.tensor_tensor(
-                out=q_sin[:].rearrange("p h (t d) -> p h t d", t=2),
-                in0=q[:].rearrange("p h (t d) -> p h t d", t=2)[:, :, ::-1, :],
-                in1=tabs[:, 1:2, :].rearrange("p o (t d) -> p o t d", t=2).to_broadcast([P, GROUP, 2, HALF]),
-                op=MULT,
-            )
-            return q_sin
-
-        def products(q, tabs):
-            return times_cos(q, tabs), times_sin(q, tabs)
-
-        def add_and_store(pair, target, adder):
-            result = work.tile([P, GROUP, HD], F32, tag="result")
-            adder.tensor_tensor(
-                out=result[:].rearrange("p h d -> p (h d)"),
-                in0=pair[0][:].rearrange("p h d -> p (h d)"),
-                in1=pair[1][:].rearrange("p h d -> p (h d)"),
+                out=q[:].rearrange("p h d -> p (h d)"),
+                in0=acc[:],
+                in1=row_bias[c][:, hh * HD : (hh + count) * HD],
                 op=ADD,
             )
-            nc.sync.dma_start(out=target, in_=result[:])
+            return q[:]
 
-        def row_target(b, c):
-            return out[b, c * GROUP : (c + 1) * GROUP, :, :].rearrange("h s d -> s h d")
+        def new_products(count):
+            q_cos = work.tile([P, count, HD], F32, tag="q_cos")
+            q_sin = work.tile([P, count, HD], F32, tag="q_sin")
+            return q_cos[:], q_sin[:]
+
+        def times_cos(q_cos, q, tabs):
+            count = q.shape[1]
+            nc.vector.tensor_tensor(out=q_cos, in0=q, in1=tabs[:, 0:1, :].to_broadcast([P, count, HD]), op=MULT)
+
+        def times_sin(q_sin, q, tabs):
+            count = q.shape[1]
+            nc.vector.tensor_tensor(
+                out=q_sin.rearrange("p h (t d) -> p h t d", t=2),
+                in0=q.rearrange("p h (t d) -> p h t d", t=2)[:, :, ::-1, :],
+                in1=tabs[:, 1:2, :].rearrange("p o (t d) -> p o t d", t=2).to_broadcast([P, count, 2, HALF]),
+                op=MULT,
+            )
+
+        def products(q, tabs):
+            pair = new_products(q.shape[1])
+            times_cos(pair[0], q, tabs)
+            times_sin(pair[1], q, tabs)
+            return pair
+
+        def add_and_store(pair, targets, adder, result=None):
+            if result is None:
+                result_tile = work.tile([P, pair[0].shape[1], HD], F32, tag="result")
+                result = result_tile[:]
+            adder.tensor_tensor(
+                out=result.rearrange("p h d -> p (h d)"),
+                in0=pair[0].rearrange("p h d -> p (h d)"),
+                in1=pair[1].rearrange("p h d -> p (h d)"),
+                op=ADD,
+            )
+            width = pair[0].shape[1] // len(targets)
+            for j, target in enumerate(targets):
+                nc.sync.dma_start(out=target, in_=result[:, j * width : (j + 1) * width, :])
+
+        def row_target(b, first, count):
+            return out[b, first : first + count, :, :].rearrange("h s d -> s h d")
 
         def col_target(j):
             return out[:, ROW_HEADS + j, :, :].rearrange("b s d -> s b d")
 
-        def finish_rows(q, b, c):
-            add_and_store(products(q, tables_ps), row_target(b, c), nc.gpsimd)
+        def finish_rows(q, b, first, count, adder):
+            add_and_store(products(q, tables_ps), [row_target(b, first, count)], adder)
 
-        def finish_cols(q, j, adder):
-            add_and_store(products(q, tables), col_target(j), adder)
+        def finish_cols(turned, heads):
+            pair = new_products(len(heads) * B)
+            for j, q in enumerate(turned):
+                times_cos(pair[0][:, j * B : (j + 1) * B, :], q[:], tables)
+                times_sin(pair[1][:, j * B : (j + 1) * B, :], q[:], tables)
+            add_and_store(pair, [col_target(j) for j in heads], nc.gpsimd)
 
+        def spread_tables():
+            nc.tensor.matmul(
+                tables_ps[:].rearrange("p t d -> p (t d)"),
+                lhsT=ident_bf16[:],
+                rhs=tables[:].rearrange("p t d -> p (t d)"),
+                start=True,
+                stop=True,
+            )
+
+        warm = psum_acc.tile([P, BANK], F32, tag="acc")
+        for i in range(4):
+            nc.tensor.matmul(warm[:], lhsT=zeros[:, 0:P], rhs=zeros[:], start=True, stop=True)
         turn_query(0, 0, 2)
-        turn_query(0, 2, 1)
-        turn_query(0, 3, 1)
+        turn_query(0, 2, 2)
         spread_row_bias(0)
         spread_row_bias(1)
-        quantize(0)
-        acc = project_rows(0, 0)
-        nc.tensor.matmul(
-            tables_ps[:].rearrange("p t d -> p (t d)"),
-            lhsT=ident_bf16[:],
-            rhs=tables[:].rearrange("p t d -> p (t d)"),
-            start=True,
-            stop=True,
-        )
-        turn_batch(1)
-        first_pair = products(add_row_bias(acc, 0), tables_ps)
-        quantize(1)
-
-        for b, c, nxt in [(0, 1, 2), (1, 0, 3)]:
-            acc = project_rows(b, c)
-            turn_batch(nxt)
-            q = add_row_bias(acc, c)
-            if first_pair is not None:
-                add_and_store(first_pair, row_target(0, 0), nc.vector)
-                first_pair = None
-            q_cos = times_cos(q, tables_ps)
-            quantize(nxt)
-            add_and_store((q_cos, times_sin(q, tables_ps)), row_target(b, c), nc.gpsimd)
         turn_col_bias()
+        turn_batch(1)
+        quantize(0)
+        quantize(1)
+        acc = project_rows(0, 0, 4)
+        spread_tables()
+        finish_rows(add_row_bias(acc, 0, 4), 0, 0, 4, nc.gpsimd)
+        for b, first, nxt in [(1, 0, 2), (0, 4, 3)]:
+            acc = project_rows(b, first, 4)
+            turn_batch(nxt)
+            q = add_row_bias(acc, first, 4)
+            pair = new_products(4)
+            times_cos(pair[0], q, tables_ps)
+            quantize(nxt)
+            times_sin(pair[1], q, tables_ps)
+            add_and_store(pair, [row_target(b, first, 4)], nc.gpsimd)
 
-        lead = [(1, 1), (2, 0)]
-        rest = [(2, 1), (3, 0), (3, 1)]
         waiting = None
-        for b, c in lead:
-            q = add_row_bias(project_rows(b, c), c)
+        for b, first, count in [(1,4,4),(2,0,4)]:
+            q = add_row_bias(project_rows(b, first, count), first, count)
             if waiting is not None:
-                finish_rows(*waiting)
-            waiting = (q, b, c)
-
+                finish_rows(*waiting, nc.gpsimd)
+            waiting = (q, b, first, count)
+        rest = [(2,4,4),(3,0,4),(3,4,4)]
         for k in range(COL_HEADS // 2):
             heads = (2 * k, 2 * k + 1)
             q_cols = [project_cols(j) for j in heads]
             if waiting is not None:
-                finish_rows(*waiting)
+                finish_rows(*waiting, nc.gpsimd)
                 waiting = None
             if k < len(rest):
-                b, c = rest[k]
-                waiting = (add_row_bias(project_rows(b, c), c), b, c)
+                b, first, count = rest[k]
+                waiting = (add_row_bias(project_rows(b, first, count), first, count), b, first, count)
             turned = [turn_back(x) for x in q_cols]
             if k < len(rest):
                 for j in range(2):
-                    finish_cols(turned[j], heads[j], nc.gpsimd)
+                    finish_cols(turned[j : j + 1], heads[j : j + 1])
             else:
-                pairs = [products(x, tables) for x in turned]
+                pairs = [products(x[:], tables) for x in turned]
                 for j in range(2):
-                    add_and_store(pairs[j], col_target(heads[j]), nc.vector)
+                    add_and_store(pairs[j], [col_target(heads[j])], nc.vector)

@@ -44,13 +44,14 @@ def tile_attention_pa_kernel(tc, query, wq_words, wq_scales, bq, cos, sin, out):
         col_scales = keep.tile([P, PASSES, COL_HEADS * HD], U8, align_bytes=64)
         w_codes = [keep.tile([P, PASSES, 2 * BANK], U8, name="w_codes%d" % c, align_bytes=64) for c in range(CHUNKS)]
         q_rows = [keep.tile([P, DIM], BF16, name="q_rows%d" % b, align_bytes=64) for b in range(B)]
-        q_grouped = keep.tile([P, PASSES, B * S * 4], BF16, align_bytes=64)
+        q_grouped = [keep.tile([P, PASSES, S * 4], BF16, name="q_grouped%d" % b, align_bytes=64) for b in range(B)]
         q_codes = keep.tile([P, PASSES, B * S], U32, align_bytes=64)
         q_scales = keep.tile([P, PASSES, B * S], U8, align_bytes=64)
         row_bias = [keep.tile([P, BANK], BF16, name="row_bias%d" % c, align_bytes=64) for c in range(ROW_CHUNKS)]
         col_bias = keep.tile([P, COL_HEADS], F32, align_bytes=64)
         bias_rows = keep.tile([P, HD], BF16, align_bytes=64)
         tables = keep.tile([P, 2, HD], BF16, align_bytes=64)
+        col_tables = keep.tile([P, 2, 4, HD], BF16, align_bytes=64)
         ident_f32 = keep.tile([P, P], F32, align_bytes=64)
         ident_bf16 = keep.tile([P, P], BF16, align_bytes=64)
         tables_ps = psum_keep.tile([P, 2, HD], F32)
@@ -70,12 +71,10 @@ def tile_attention_pa_kernel(tc, query, wq_words, wq_scales, bq, cos, sin, out):
                 nc.sync.dma_start(out=q_rows[b][:, cols], in_=query[b, :, cols])
 
         def load_scales(plane, first, count):
-            for quad in range(4):
+            for r in range(4):
                 nc.sync.dma_start(
-                    out=plane[32 * quad : 32 * quad + 4, :, :].bitcast(I32),
-                    in_=wq_scales[:, 4 * quad : 4 * quad + 4, first * BANK : (first + count) * BANK]
-                    .rearrange("g r n -> r g n")
-                    .bitcast(I32),
+                    out=plane[r:P:32, :, :].bitcast(I32),
+                    in_=wq_scales[:, r:16:4, first * BANK : (first + count) * BANK].rearrange("g q n -> q g n").bitcast(I32),
                 )
 
         def load_codes(c, pieces):
@@ -101,10 +100,14 @@ def tile_attention_pa_kernel(tc, query, wq_words, wq_scales, bq, cos, sin, out):
         load_codes(1, 1)
         load_query(3, 1)
         load_scales(col_scales, ROW_CHUNKS, CHUNKS - ROW_CHUNKS)
-        for c in range(ROW_CHUNKS, CHUNKS):
+        load_codes(ROW_CHUNKS, 1)
+        for t, table in enumerate((cos, sin)):
+            nc.sync.dma_start(
+                out=col_tables[:, t, :, :].rearrange("p j d -> p (j d)"),
+                in_=table[0, 0].rearrange("(i o j) d -> i o (j d)", o=1, j=4).to_broadcast([S // 4, B, 4 * HD]),
+            )
+        for c in range(ROW_CHUNKS + 1, CHUNKS):
             load_codes(c, 1)
-
-        grouped_words = q_grouped[:].bitcast(F32).rearrange("p g (b s u) -> p g b s u", b=B, u=2)
 
         def turn_query(b, first, count):
             words = q_rows[b][:].bitcast(F32)
@@ -114,7 +117,8 @@ def tile_attention_pa_kernel(tc, query, wq_words, wq_scales, bq, cos, sin, out):
                 for u in range(2):
                     nc.tensor.transpose(turned[:, j, u, :], words[:, 256 * g + u : 256 * (g + 1) : 2], ident_f32[:])
             nc.scalar.copy(
-                out=grouped_words[:, first : first + count, b], in_=turned[:].rearrange("p j u s -> p j s u")
+                out=q_grouped[b][:, first : first + count, :].bitcast(F32).rearrange("p j (s u) -> p j s u", u=2),
+                in_=turned[:].rearrange("p j u s -> p j s u"),
             )
 
         def turn_batch(b):
@@ -127,7 +131,7 @@ def tile_attention_pa_kernel(tc, query, wq_words, wq_scales, bq, cos, sin, out):
                 nc.vector.quantize_mx(
                     out=q_codes[:, g, cols].bitcast(FP8X4),
                     scales=q_scales[:, g, cols],
-                    in_=q_grouped[:, g, 4 * b * S : 4 * (b + 1) * S],
+                    in_=q_grouped[b][:, g, :],
                 )
 
         def spread_row_bias(c):
@@ -178,7 +182,10 @@ def tile_attention_pa_kernel(tc, query, wq_words, wq_scales, bq, cos, sin, out):
                 )
             q_cols = work.tile([P, B, S], F32, tag="q_cols")
             nc.scalar.activation(
-                out=q_cols[:].rearrange("p b s -> p (b s)"), in_=acc[:], func=IDENTITY, bias=col_bias[:, j : j + 1]
+                out=q_cols[:].rearrange("p j (i b) -> p j i b", b=B),
+                in_=acc[:].rearrange("p (b i j) -> p j i b", b=B, j=4),
+                func=IDENTITY,
+                bias=col_bias[:, j : j + 1],
             )
             return q_cols
 
@@ -204,16 +211,20 @@ def tile_attention_pa_kernel(tc, query, wq_words, wq_scales, bq, cos, sin, out):
             q_sin = work.tile([P, count, HD], F32, tag="q_sin")
             return q_cos[:], q_sin[:]
 
+        row_tabs = (
+            tables_ps[:, 0:1, :].to_broadcast([P, GROUP, HD]),
+            tables_ps[:, 1:2, :].rearrange("p o (t d) -> p o t d", t=2).to_broadcast([P, GROUP, 2, HALF]),
+        )
+        col_tabs = (col_tables[:, 0, :, :], col_tables[:, 1, :, :].rearrange("p j (t d) -> p j t d", t=2))
+
         def times_cos(q_cos, q, tabs):
-            count = q.shape[1]
-            nc.vector.tensor_tensor(out=q_cos, in0=q, in1=tabs[:, 0:1, :].to_broadcast([P, count, HD]), op=MULT)
+            nc.vector.tensor_tensor(out=q_cos, in0=q, in1=tabs[0], op=MULT)
 
         def times_sin(q_sin, q, tabs):
-            count = q.shape[1]
             nc.vector.tensor_tensor(
                 out=q_sin.rearrange("p h (t d) -> p h t d", t=2),
                 in0=q.rearrange("p h (t d) -> p h t d", t=2)[:, :, ::-1, :],
-                in1=tabs[:, 1:2, :].rearrange("p o (t d) -> p o t d", t=2).to_broadcast([P, count, 2, HALF]),
+                in1=tabs[1],
                 op=MULT,
             )
 
@@ -235,22 +246,23 @@ def tile_attention_pa_kernel(tc, query, wq_words, wq_scales, bq, cos, sin, out):
             )
             width = pair[0].shape[1] // len(targets)
             for j, target in enumerate(targets):
-                nc.sync.dma_start(out=target, in_=result[:, j * width : (j + 1) * width, :])
+                part = result[:, j * width : (j + 1) * width, :]
+                nc.sync.dma_start(out=target, in_=part if target.shape[0] == P else part.rearrange("p j d -> p (j d)"))
 
         def row_target(b, first, count):
             return out[b, first : first + count, :, :].rearrange("h s d -> s h d")
 
         def col_target(j):
-            return out[:, ROW_HEADS + j, :, :].rearrange("b s d -> s b d")
+            return out[:, ROW_HEADS + j, :, :].rearrange("b (i j) d -> i b (j d)", j=4)
 
         def finish_rows(q, b, first, count, adder):
-            add_and_store(products(q, tables_ps), [row_target(b, first, count)], adder)
+            add_and_store(products(q, row_tabs), [row_target(b, first, count)], adder)
 
         def finish_cols(turned, heads):
             pair = new_products(len(heads) * B)
             for j, q in enumerate(turned):
-                times_cos(pair[0][:, j * B : (j + 1) * B, :], q[:], tables)
-                times_sin(pair[1][:, j * B : (j + 1) * B, :], q[:], tables)
+                times_cos(pair[0][:, j * B : (j + 1) * B, :], q[:], col_tabs)
+                times_sin(pair[1][:, j * B : (j + 1) * B, :], q[:], col_tabs)
             add_and_store(pair, [col_target(j) for j in heads], nc.gpsimd)
 
         def spread_tables():
@@ -275,38 +287,52 @@ def tile_attention_pa_kernel(tc, query, wq_words, wq_scales, bq, cos, sin, out):
         quantize(1)
         acc = project_rows(0, 0, 4)
         spread_tables()
-        finish_rows(add_row_bias(acc, 0, 4), 0, 0, 4, nc.gpsimd)
-        for b, first, nxt in [(1, 0, 2), (0, 4, 3)]:
+        q = add_row_bias(acc, 0, 4)
+        pair = new_products(4)
+        times_cos(pair[0], q, row_tabs)
+        waiting = (q, pair, 0, 0)
+        for b, first, nxt in [(1, 0, 2), (0, 4, 3), (1, 4, None)]:
             acc = project_rows(b, first, 4)
-            turn_batch(nxt)
+            if nxt is not None:
+                turn_batch(nxt)
             q = add_row_bias(acc, first, 4)
+            times_sin(waiting[1][1], waiting[0], row_tabs)
             pair = new_products(4)
-            times_cos(pair[0], q, tables_ps)
-            quantize(nxt)
-            times_sin(pair[1], q, tables_ps)
-            add_and_store(pair, [row_target(b, first, 4)], nc.gpsimd)
+            if nxt is not None:
+                times_cos(pair[0], q, row_tabs)
+                quantize(nxt)
+                spent = q_grouped[nxt][:, 2:4, :].rearrange("p g x -> p (g x)").bitcast(F32)
+                add_and_store(waiting[1], [row_target(waiting[2], waiting[3], 4)], nc.gpsimd, spent.rearrange("p (h d) -> p h d", d=HD))
+            else:
+                add_and_store(waiting[1], [row_target(waiting[2], waiting[3], 4)], nc.gpsimd)
+            waiting = (q, pair, b, first)
+        first_waiting = (q, b, first, 4)
+        nc.scalar.activation(out=col_tables[:, 1, :, 0:HALF], in_=col_tables[:, 1, :, 0:HALF], func=IDENTITY, scale=-1.0)
 
-        waiting = None
-        for b, first, count in [(1,4,4),(2,0,4)]:
-            q = add_row_bias(project_rows(b, first, count), first, count)
+        waiting = first_waiting
+        for b, first in [(2,0),(2,4)]:
+            q = add_row_bias(project_rows(b, first, 4), first, 4)
             if waiting is not None:
                 finish_rows(*waiting, nc.gpsimd)
-            waiting = (q, b, first, count)
-        rest = [(2,4,4),(3,0,4),(3,4,4)]
+            waiting = (q, b, first, 4)
+        rest = [(3,0),(3,4)]
+        q_cols = []
         for k in range(COL_HEADS // 2):
             heads = (2 * k, 2 * k + 1)
-            q_cols = [project_cols(j) for j in heads]
+            q_cols.extend([project_cols(j) for j in range(len(q_cols), 2 * k + 2)])
             if waiting is not None:
                 finish_rows(*waiting, nc.gpsimd)
                 waiting = None
             if k < len(rest):
-                b, first, count = rest[k]
-                waiting = (add_row_bias(project_rows(b, first, count), first, count), b, first, count)
-            turned = [turn_back(x) for x in q_cols]
-            if k < len(rest):
+                b, first = rest[k]
+                waiting = (add_row_bias(project_rows(b, first, 4), first, 4), b, first, 4)
+            elif len(q_cols) < COL_HEADS:
+                q_cols.append(project_cols(len(q_cols)))
+            turned = [turn_back(q_cols[j]) for j in heads]
+            if k + 1 < COL_HEADS // 2:
                 for j in range(2):
                     finish_cols(turned[j : j + 1], heads[j : j + 1])
             else:
-                pairs = [products(x[:], tables) for x in turned]
+                pairs = [products(x[:], col_tabs) for x in turned]
                 for j in range(2):
                     add_and_store(pairs[j], [col_target(heads[j])], nc.vector)

from contextlib import ExitStack

import concourse.mybir as mybir
from concourse.masks import make_identity

B, S, DIM, H, HD = 4, 128, 2048, 16, 128
E = H * HD
FLOPS = 2 * B * S * DIM * E

F32 = mybir.dt.float32
BF16 = mybir.dt.bfloat16
I32 = mybir.dt.int32
U32 = mybir.dt.uint32
U8 = mybir.dt.uint8
FP8X4 = mybir.dt.float8_e5m2_x4
FP4X4 = mybir.dt.float4_e2m1fn_x4
ADD = mybir.AluOpType.add
MULT = mybir.AluOpType.mult
IDENTITY = mybir.ActivationFunctionType.Identity

P = 128
PASSES = DIM // 512
BANK = 512
GROUP = BANK // HD
HALF = HD // 2
CHUNKS = E // BANK
ROW_CHUNKS = 2
ROW_HEADS = ROW_CHUNKS * GROUP
COL_HEADS = H - ROW_HEADS


def tile_attention_pa_kernel(tc, query, wq_words, wq_scales, bq, cos, sin, out):
    nc = tc.nc

    with ExitStack() as ctx:
        keep = ctx.enter_context(tc.tile_pool(name="keep", bufs=1))
        work = ctx.enter_context(tc.tile_pool(name="work", bufs=4))
        psum_keep = ctx.enter_context(tc.psum_pool(name="psum_keep", bufs=1))
        psum_turn = ctx.enter_context(tc.psum_pool(name="psum_turn", bufs=3))
        psum_acc = ctx.enter_context(tc.psum_pool(name="psum_acc", bufs=4))
        ctx.enter_context(tc.manual_schedule())

        row_scales = [keep.tile([P, PASSES, BANK], U8, name="row_scales%d" % c, align_bytes=64) for c in range(ROW_CHUNKS)]
        col_scales = keep.tile([P, PASSES, COL_HEADS * HD], U8, align_bytes=64)
        w_codes = [keep.tile([P, PASSES, 2 * BANK], U8, name="w_codes%d" % c, align_bytes=64) for c in range(CHUNKS)]
        q_rows = [keep.tile([P, DIM], BF16, name="q_rows%d" % b, align_bytes=64) for b in range(B)]
        q_grouped = [keep.tile([P, PASSES, S * 4], BF16, name="q_grouped%d" % b, align_bytes=64) for b in range(B)]
        q_codes = keep.tile([P, PASSES, B * S], U32, align_bytes=64)
        q_scales = keep.tile([P, PASSES, B * S], U8, align_bytes=64)
        row_bias = [keep.tile([P, BANK], BF16, name="row_bias%d" % c, align_bytes=64) for c in range(ROW_CHUNKS)]
        col_bias = keep.tile([P, COL_HEADS], F32, align_bytes=64)
        bias_rows = keep.tile([P, HD], BF16, align_bytes=64)
        tables = keep.tile([P, 2, HD], BF16, align_bytes=64)
        col_tables = keep.tile([P, 2, 4, HD], BF16, align_bytes=64)
        ident_f32 = keep.tile([P, P], F32, align_bytes=64)
        ident_bf16 = keep.tile([P, P], BF16, align_bytes=64)
        tables_ps = psum_keep.tile([P, 2, HD], F32)

        zeros = keep.tile([P, BANK], BF16, align_bytes=64)
        nc.vector.memset(zeros[:].bitcast(I32), 0)
        nc.vector.memset(bias_rows[:].bitcast(I32), 0)
        nc.vector.memset(row_scales[0][:].bitcast(I32), 0)
        make_identity(nc, ident_f32[:])
        nc.vector.memset(row_scales[1][:].bitcast(I32), 0)
        nc.vector.tensor_copy(out=ident_bf16[:], in_=ident_f32[:])
        nc.vector.memset(col_scales[:].bitcast(I32), 0)

        def load_query(b, pieces):
            for j in range(pieces):
                cols = slice(j * DIM // pieces, (j + 1) * DIM // pieces)
                nc.sync.dma_start(out=q_rows[b][:, cols], in_=query[b, :, cols])

        def load_scales(plane, first, count):
            for r in range(4):
                nc.sync.dma_start(
                    out=plane[r:P:32, :, :].bitcast(I32),
                    in_=wq_scales[:, r:16:4, first * BANK : (first + count) * BANK].rearrange("g q n -> q g n").bitcast(I32),
                )

        def load_codes(c, pieces):
            for j in range(pieces):
                passes = slice(j * PASSES // pieces, (j + 1) * PASSES // pieces)
                nc.sync.dma_start(
                    out=w_codes[c][:, passes, :].bitcast(I32),
                    in_=wq_words[passes, :, 2 * c * BANK : 2 * (c + 1) * BANK].rearrange("g p n -> p g n").bitcast(I32),
                )

        load_query(0, 2)
        nc.sync.dma_start(out=bias_rows[0:H, :], in_=bq.rearrange("(h d) -> h d", d=HD))
        nc.sync.dma_start(out=tables[:, 1, :], in_=sin[0, 0])
        nc.vector.tensor_scalar(
            out=tables[:, 1, 0:HALF], in0=tables[:, 1, 0:HALF], scalar1=-1.0, scalar2=None, op0=MULT
        )
        load_query(1, 1)
        load_scales(row_scales[0], 0, 1)
        load_codes(0, 2)
        nc.sync.dma_start(out=tables[:, 0, :], in_=cos[0, 0])
        load_query(2, 1)
        load_scales(row_scales[1], 1, 1)
        load_codes(1, 1)
        load_query(3, 1)
        load_scales(col_scales, ROW_CHUNKS, CHUNKS - ROW_CHUNKS)
        load_codes(ROW_CHUNKS, 1)
        for t, table in enumerate((cos, sin)):
            nc.sync.dma_start(
                out=col_tables[:, t, :, :].rearrange("p j d -> p (j d)"),
                in_=table[0, 0].rearrange("(i o j) d -> i o (j d)", o=1, j=4).to_broadcast([S // 4, B, 4 * HD]),
            )
        for c in range(ROW_CHUNKS + 1, CHUNKS):
            load_codes(c, 1)

        def turn_query(b, first, count):
            words = q_rows[b][:].bitcast(F32)
            turned = psum_turn.tile([P, count, 2, S], F32, tag="turn")
            for j in range(count):
                g = first + j
                for u in range(2):
                    nc.tensor.transpose(turned[:, j, u, :], words[:, 256 * g + u : 256 * (g + 1) : 2], ident_f32[:])
            nc.scalar.copy(
                out=q_grouped[b][:, first : first + count, :].bitcast(F32).rearrange("p j (s u) -> p j s u", u=2),
                in_=turned[:].rearrange("p j u s -> p j s u"),
            )

        def turn_batch(b):
            turn_query(b, 0, 2)
            turn_query(b, 2, 2)

        def quantize(b):
            cols = slice(b * S, (b + 1) * S)
            for g in range(PASSES):
                nc.vector.quantize_mx(
                    out=q_codes[:, g, cols].bitcast(FP8X4),
                    scales=q_scales[:, g, cols],
                    in_=q_grouped[b][:, g, :],
                )

        def spread_row_bias(c):
            spread = psum_acc.tile([P, GROUP, HD], BF16, tag="acc")
            for hh in range(GROUP):
                h = c * GROUP + hh
                nc.tensor.matmul(
                    spread[:, hh, :],
                    lhsT=ident_bf16[:, h : h + 1].to_broadcast([P, P]),
                    rhs=bias_rows[:],
                    start=True,
                    stop=True,
                )
            nc.scalar.copy(out=row_bias[c][:], in_=spread[:].rearrange("p h d -> p (h d)"))

        def turn_col_bias():
            turned = psum_acc.tile([P, COL_HEADS], F32, tag="acc")
            nc.tensor.matmul(turned[:], lhsT=bias_rows[:], rhs=ident_bf16[:, ROW_HEADS:H], start=True, stop=True)
            nc.scalar.copy(out=col_bias[:], in_=turned[:])

        def project_rows(b, first, count):
            c, hh = divmod(first, GROUP)
            acc = psum_acc.tile([P, count * HD], F32, tag="acc")
            for g in range(PASSES):
                nc.tensor.matmul_mx(
                    out=acc[:],
                    lhsT=q_codes[:, g, b * S : (b + 1) * S].bitcast(FP8X4),
                    lhsT_scale=q_scales[:, g, b * S : (b + 1) * S],
                    rhs=w_codes[c][:, g, 2 * hh * HD : 2 * (hh + count) * HD].bitcast(FP4X4),
                    rhs_scale=row_scales[c][:, g, hh * HD : (hh + count) * HD],
                    start=(g == 0),
                    stop=(g == PASSES - 1),
                )
            return acc

        def project_cols(j):
            c, hh = divmod(ROW_HEADS + j, GROUP)
            acc = psum_acc.tile([P, BANK], F32, tag="acc")
            for g in range(PASSES):
                nc.tensor.matmul_mx(
                    out=acc[:],
                    lhsT=w_codes[c][:, g, 2 * hh * HD : 2 * (hh + 1) * HD].bitcast(FP4X4),
                    lhsT_scale=col_scales[:, g, j * HD : (j + 1) * HD],
                    rhs=q_codes[:, g, :].bitcast(FP8X4),
                    rhs_scale=q_scales[:, g, :],
                    start=(g == 0),
                    stop=(g == PASSES - 1),
                )
            q_cols = work.tile([P, B, S], F32, tag="q_cols")
            nc.scalar.activation(
                out=q_cols[:].rearrange("p j (i b) -> p j i b", b=B),
                in_=acc[:].rearrange("p (b i j) -> p j i b", b=B, j=4),
                func=IDENTITY,
                bias=col_bias[:, j : j + 1],
            )
            return q_cols

        def turn_back(q_cols):
            q = psum_turn.tile([P, B, HD], F32, tag="turn")
            for b in range(B):
                nc.tensor.transpose(q[:, b, :], q_cols[:, b, :], ident_f32[:])
            return q

        def add_row_bias(acc, first, count):
            c, hh = divmod(first, GROUP)
            q = work.tile([P, count, HD], F32, tag="q")
            nc.vector.tensor_tensor(
                out=q[:].rearrange("p h d -> p (h d)"),
                in0=acc[:],
                in1=row_bias[c][:, hh * HD : (hh + count) * HD],
                op=ADD,
            )
            return q[:]

        def new_products(count):
            q_cos = work.tile([P, count, HD], F32, tag="q_cos")
            q_sin = work.tile([P, count, HD], F32, tag="q_sin")
            return q_cos[:], q_sin[:]

        row_tabs = (
            tables_ps[:, 0:1, :].to_broadcast([P, GROUP, HD]),
            tables_ps[:, 1:2, :].rearrange("p o (t d) -> p o t d", t=2).to_broadcast([P, GROUP, 2, HALF]),
        )
        col_tabs = (col_tables[:, 0, :, :], col_tables[:, 1, :, :].rearrange("p j (t d) -> p j t d", t=2))

        def times_cos(q_cos, q, tabs):
            nc.vector.tensor_tensor(out=q_cos, in0=q, in1=tabs[0], op=MULT)

        def times_sin(q_sin, q, tabs):
            nc.vector.tensor_tensor(
                out=q_sin.rearrange("p h (t d) -> p h t d", t=2),
                in0=q.rearrange("p h (t d) -> p h t d", t=2)[:, :, ::-1, :],
                in1=tabs[1],
                op=MULT,
            )

        def products(q, tabs):
            pair = new_products(q.shape[1])
            times_cos(pair[0], q, tabs)
            times_sin(pair[1], q, tabs)
            return pair

        def add_and_store(pair, targets, adder, result=None):
            if result is None:
                result_tile = work.tile([P, pair[0].shape[1], HD], F32, tag="result")
                result = result_tile[:]
            adder.tensor_tensor(
                out=result.rearrange("p h d -> p (h d)"),
                in0=pair[0].rearrange("p h d -> p (h d)"),
                in1=pair[1].rearrange("p h d -> p (h d)"),
                op=ADD,
            )
            width = pair[0].shape[1] // len(targets)
            for j, target in enumerate(targets):
                part = result[:, j * width : (j + 1) * width, :]
                nc.sync.dma_start(out=target, in_=part if target.shape[0] == P else part.rearrange("p j d -> p (j d)"))

        def row_target(b, first, count):
            return out[b, first : first + count, :, :].rearrange("h s d -> s h d")

        def col_target(j):
            return out[:, ROW_HEADS + j, :, :].rearrange("b (i j) d -> i b (j d)", j=4)

        def finish_rows(q, b, first, count, adder):
            add_and_store(products(q, row_tabs), [row_target(b, first, count)], adder)

        def finish_cols(turned, heads):
            pair = new_products(len(heads) * B)
            for j, q in enumerate(turned):
                times_cos(pair[0][:, j * B : (j + 1) * B, :], q[:], col_tabs)
                times_sin(pair[1][:, j * B : (j + 1) * B, :], q[:], col_tabs)
            add_and_store(pair, [col_target(j) for j in heads], nc.gpsimd)

        def spread_tables():
            nc.tensor.matmul(
                tables_ps[:].rearrange("p t d -> p (t d)"),
                lhsT=ident_bf16[:],
                rhs=tables[:].rearrange("p t d -> p (t d)"),
                start=True,
                stop=True,
            )

        warm = psum_acc.tile([P, BANK], F32, tag="acc")
        for i in range(4):
            nc.tensor.matmul(warm[:], lhsT=zeros[:, 0:P], rhs=zeros[:], start=True, stop=True)
        turn_query(0, 0, 2)
        turn_query(0, 2, 2)
        spread_row_bias(0)
        spread_row_bias(1)
        turn_col_bias()
        turn_batch(1)
        quantize(0)
        quantize(1)
        acc = project_rows(0, 0, 4)
        spread_tables()
        q = add_row_bias(acc, 0, 4)
        pair = new_products(4)
        times_cos(pair[0], q, row_tabs)
        waiting = (q, pair, 0, 0)
        for b, first, nxt in [(1, 0, 2), (0, 4, 3), (1, 4, None)]:
            acc = project_rows(b, first, 4)
            if nxt is not None:
                turn_batch(nxt)
            q = add_row_bias(acc, first, 4)
            times_sin(waiting[1][1], waiting[0], row_tabs)
            pair = new_products(4)
            if nxt is not None:
                times_cos(pair[0], q, row_tabs)
                quantize(nxt)
                spent = q_grouped[nxt][:, 2:4, :].rearrange("p g x -> p (g x)").bitcast(F32)
                add_and_store(waiting[1], [row_target(waiting[2], waiting[3], 4)], nc.gpsimd, spent.rearrange("p (h d) -> p h d", d=HD))
            else:
                add_and_store(waiting[1], [row_target(waiting[2], waiting[3], 4)], nc.gpsimd)
            waiting = (q, pair, b, first)
        first_waiting = (q, b, first, 4)
        nc.scalar.activation(out=col_tables[:, 1, :, 0:HALF], in_=col_tables[:, 1, :, 0:HALF], func=IDENTITY, scale=-1.0)

        waiting = first_waiting
        for b, first in [(2,0),(2,4)]:
            q = add_row_bias(project_rows(b, first, 4), first, 4)
            if waiting is not None:
                finish_rows(*waiting, nc.gpsimd)
            waiting = (q, b, first, 4)
        rest = [(3,0),(3,4)]
        q_cols = []
        for k in range(COL_HEADS // 2):
            heads = (2 * k, 2 * k + 1)
            q_cols.extend([project_cols(j) for j in range(len(q_cols), 2 * k + 2)])
            if waiting is not None:
                finish_rows(*waiting, nc.gpsimd)
                waiting = None
            if k < len(rest):
                b, first = rest[k]
                waiting = (add_row_bias(project_rows(b, first, 4), first, 4), b, first, 4)
            elif len(q_cols) < COL_HEADS:
                q_cols.append(project_cols(len(q_cols)))
            turned = [turn_back(q_cols[j]) for j in heads]
            if k + 1 < COL_HEADS // 2:
                for j in range(2):
                    finish_cols(turned[j : j + 1], heads[j : j + 1])
            else:
                pairs = [products(x[:], col_tabs) for x in turned]
                for j in range(2):
                    add_and_store(pairs[j], [col_target(heads[j])], nc.vector)
